import numpy as np
import ml_dtypes


def mxq(x, axis, fmt="e4m3"):
    dtype, down = {"e4m3": (ml_dtypes.float8_e4m3fn, 7), "e5m2": (ml_dtypes.float8_e5m2, 14)}[fmt]
    v = np.moveaxis(np.asarray(x, np.float32).astype(ml_dtypes.bfloat16).astype(np.float64), axis, -1)
    blocks = v.reshape(v.shape[:-1] + (-1, 32))
    amax = np.abs(blocks).max(-1, keepdims=True)
    byte = np.maximum(np.where(amax > 0, np.frexp(amax)[1] - 1 + 127, 0) - down, 1)
    scale = np.exp2(byte - 127.0)
    codes = (blocks / scale).astype(np.float32).astype(dtype).astype(np.float64)
    return np.moveaxis((codes * scale).reshape(v.shape), -1, axis)


WIDE = False


def mx_kscale(k):
    if not WIDE:
        return np.ones(k)
    levels = np.array([10, -10, 5, -5, 0])
    if k % 512:
        return np.exp2(np.random.permutation(np.resize(levels, k // 32))).repeat(32)
    a = np.empty((k // 512, 16))
    for p in range(k // 512):
        a[p, :8] = np.random.permutation(np.resize(levels, 8))
        for g in range(8):
            far = levels[np.abs(levels - a[p, g]) >= 10]
            a[p, g + 8] = far[np.random.randint(len(far))]
    return np.exp2(a.ravel()).repeat(32)


BF16 = ml_dtypes.bfloat16


def bf(x):
    return np.asarray(x, np.float32).astype(BF16)


def f64(x):
    return np.asarray(x).astype(np.float64)


B, C, H, W, O, KH, KW, PH, PW, T, R = 4, 1024, 7, 7, 512, 2, 2, 1, 1, 8, 64
HO, WO = H + PH + PH - KH + 1, W + PW + PW - KW + 1
N = B * HO * WO
D = C * KH * KW
R2 = R * KH * KW
K1, K2 = T * R, T * R2


def draw0():
    s, t1, t2 = mx_kscale(D), mx_kscale(K1).reshape(T, R), mx_kscale(K2).reshape(T, R2)
    return {"xw": bf(np.random.standard_normal((N, D)) * s),
            "S1s": bf(np.random.standard_normal((T, D, R)) / np.sqrt(D) / s[None, :, None] * t1[:, None, :]),
            "U1s": bf(np.random.standard_normal((T, R, O)) * T / np.sqrt(K1) / t1[:, :, None]),
            "U2s": bf(np.random.standard_normal((T, R2, D)) / np.sqrt(D) / s[None, None, :] * t2[:, :, None]),
            "S2s": bf(np.random.standard_normal((T, R2, O)) * T / np.sqrt(K2) / t2[:, :, None]),
            "bias": bf(np.random.standard_normal(O) * 0.3)}


def core(xw, S1s, U1s, U2s, S2s, bias):
    xq = mxq(f64(xw), 1, "e4m3")
    s1 = f64(S1s).transpose(1, 0, 2).reshape(D, K1)
    h1 = xq @ mxq(s1, 0, "e4m3")
    out1 = (mxq(h1, 1, "e4m3") @ mxq(f64(U1s).reshape(K1, O), 0, "e4m3")) / T + f64(bias)
    u2 = f64(U2s).reshape(K2, D)
    h2 = xq @ mxq(u2, 1, "e4m3").T
    out2 = (mxq(h2, 1, "e4m3") @ mxq(f64(S2s).reshape(K2, O), 0, "e4m3")) / T
    out = out1 + out2 + f64(bias)
    return out.reshape(B, HO, WO, O).transpose(0, 3, 1, 2)


def e4m3fn_bytes(y):
    return np.clip(np.asarray(y, np.float64), -448.0, 448.0).astype(np.float32).astype(ml_dtypes.float8_e4m3fn).view(np.uint8)


def e4m3fn_values(b):
    return np.asarray(b, np.uint8).view(ml_dtypes.float8_e4m3fn).astype(np.float64)


def setup_inputs():
    d = draw0()
    x0 = np.asarray(d['xw']).astype(np.float64)
    s = (np.max(np.abs(x0), axis=(0,), keepdims=True) / 448.0).astype(np.float32)
    out = {}
    for k, v in d.items():
        if k == 'xw':
            out['xw_bytes'] = e4m3fn_bytes(x0 / s.astype(np.float64))
            out['xw_scale'] = s
        else:
            out[k] = v
    return out


def reference(xw_bytes, xw_scale, S1s, U1s, U2s, S2s, bias):
    return core(e4m3fn_values(xw_bytes) * xw_scale.astype(np.float64), S1s, U1s, U2s, S2s, bias)

from contextlib import ExitStack

import concourse.mybir as mybir
from concourse.masks import make_identity

F32 = mybir.dt.float32
BF16 = mybir.dt.bfloat16
U32 = mybir.dt.uint32
U8 = mybir.dt.uint8
FP8 = mybir.dt.float8_e4m3fn
FP8X4 = mybir.dt.float8_e4m3fn_x4
MULT = mybir.AluOpType.mult
ADD = mybir.AluOpType.add
IDENTITY = mybir.ActivationFunctionType.Identity

P = 128
N = 256
D = 4096
O = 512
K1 = 512
K2 = 2048
GD = D // 512
G2 = K2 // 512
TILES = K2 // P
SEQ = [0, 2, 4, 1, 3, 5] + list(range(6, 16))

FLOPS = 2 * N * D * (K1 + K2) + 2 * N * (K1 + K2) * O


def tile_skconv2d_pa_kernel(tc, xw_bytes, xw_scale, S1s, U1s, U2s, S2s, bias, out):
    nc = tc.nc

    with ExitStack() as ctx:
        const = ctx.enter_context(tc.tile_pool(name="const", bufs=1))
        keep = ctx.enter_context(tc.tile_pool(name="keep", bufs=1))
        pool = ctx.enter_context(tc.tile_pool(name="pool", bufs=2))
        psum = ctx.enter_context(tc.psum_pool(name="psum", bufs=2))
        ctx.enter_context(tc.manual_schedule())

        u2_rows = U2s.rearrange("t r d -> (t r) d").rearrange("(g p t) d -> g t p d", p=P, t=4)
        s1_rows = S1s.rearrange("t (g p j) r -> g p t (j r)", p=P, j=4)
        s2_rows = S2s.rearrange("t r o -> (t r) o").rearrange("(g p j) o -> g p (j o)", p=P, j=4)
        u1_rows = U1s.rearrange("t r o -> (t r) o").rearrange("(g p j) o -> g p (j o)", p=P, j=4)

        ident = const.tile([P, P], F32, name="ident", align_bytes=64)
        make_identity(nc, ident[:])
        x_scale = const.tile([P, GD, 4], F32, name="x_scale", align_bytes=64)
        bias_in = const.tile([P, 4], BF16, name="bias_in", align_bytes=64)

        u2_raw = {}

        def load_u2(i, pieces=1):
            raw = pool.tile([P, D], BF16, name="u2_raw", bufs=5, align_bytes=64)
            w = D // pieces
            for c in range(pieces):
                nc.sync.dma_start(out=raw[:, c * w : (c + 1) * w], in_=u2_rows[i // 4, i % 4][:, c * w : (c + 1) * w])
            u2_raw[i] = raw

        w_raw = {}

        def load_w(c):
            raw = pool.tile([P, 2048], BF16, name="w_raw", bufs=3, align_bytes=64)
            if c < 8:
                nc.sync.dma_start(out=raw[:].rearrange("p (t x) -> p t x", t=8), in_=s1_rows[c])
            elif c < 12:
                nc.sync.dma_start(out=raw[:], in_=s2_rows[c - 8])
            else:
                nc.sync.dma_start(out=raw[:], in_=u1_rows[0])
            w_raw[c] = raw

        load_u2(SEQ[0], 4)
        x_in = []
        for h in range(2):
            xi = keep.tile([P, D], U8, name="x_in%d" % h, align_bytes=64)
            nc.sync.dma_start(out=xi[:], in_=xw_bytes[h * P : (h + 1) * P, :])
            x_in.append(xi)
        nc.sync.dma_start(out=x_scale[:], in_=xw_scale.rearrange("o (g p t) -> p (o g) t", p=P, t=4))
        load_u2(SEQ[1], 2)
        for i in range(2, 5):
            load_u2(SEQ[i])
        nc.sync.dma_start(out=bias_in[:], in_=bias.rearrange("(p m) -> p m", m=4))

        x_bf = [keep.tile([P, D], BF16, name="x_bf%d" % h, align_bytes=64) for h in range(2)]
        x_codes = keep.tile([P, GD, N], U32, name="x_codes", align_bytes=64)
        x_scales = keep.tile([P, GD, N], U8, name="x_scales", align_bytes=64)
        for q, h in [(0, 0), (0, 1), (1, 0), (1, 1), (2, 0), (2, 1), (3, 0), (3, 1)]:
            cols = slice(q * 1024, (q + 1) * 1024)
            nc.vector.tensor_copy(out=x_bf[h][:, cols], in_=x_in[h][:, cols].bitcast(FP8))

        x_grp = {}

        def turn_x(g):
            xt = psum.tile([P, 2, N], F32, name="tp", bufs=5)
            for h in range(2):
                words = x_bf[h][:].bitcast(F32)
                for u in range(2):
                    nc.tensor.transpose(
                        xt[:, u, h * P : (h + 1) * P], words[:, 256 * g + u : 256 * (g + 1) : 2], ident[:]
                    )
            if g % 2 == 0:
                x_grp[g // 2] = pool.tile([P, 2, N, 4], BF16, name="x_grp", bufs=2, align_bytes=64)
            grp = x_grp[g // 2]
            sc = x_scale[:, g : g + 1, :].rearrange("p o (u e) -> p o u e", u=2)
            nc.vector.tensor_tensor(
                out=grp[:, g % 2].rearrange("p n (u e) -> p n u e", u=2),
                in0=xt[:].rearrange("p u n -> p (u n)").bitcast(BF16).rearrange("p (u n e) -> p n u e", u=2, e=2),
                in1=sc.to_broadcast([P, N, 2, 2]),
                op=MULT,
            )

        def quant_x(b):
            nc.vector.quantize_mx(
                out=x_codes[:, 2 * b : 2 * b + 2, :].rearrange("p g n -> p (g n)").bitcast(FP8X4),
                scales=x_scales[:, 2 * b : 2 * b + 2, :].rearrange("p g n -> p (g n)"),
                in_=x_grp[b][:].rearrange("p g n t -> p (g n t)"),
            )

        u2_grp = {}
        u2_codes = {}

        def turn_u2(i, b):
            if b == 0:
                u2_grp[i] = pool.tile([P, GD, P, 4], BF16, name="u2_grp", bufs=4, align_bytes=64)
            words = u2_raw[i][:].bitcast(F32)
            ut = psum.tile([P, 2, 2, P], F32, name="tp", bufs=5)
            for s in range(2):
                g = 2 * b + s
                for u in range(2):
                    nc.tensor.transpose(ut[:, s, u, :], words[:, 256 * g + u : 256 * (g + 1) : 2], ident[:])
            nc.scalar.copy(
                out=u2_grp[i][:, 2 * b : 2 * b + 2].rearrange("p g n t -> p (g n t)").bitcast(F32)
                .rearrange("p (g n u) -> p g n u", g=2, u=2),
                in_=ut[:].rearrange("p g u n -> p g n u"),
            )

        def quant_u2(i):
            codes = pool.tile([P, GD, P], U32, name="u2_codes", bufs=5, align_bytes=64)
            scales = pool.tile([P, GD, P], U8, name="u2_scales", bufs=5, align_bytes=64)
            nc.vector.quantize_mx(
                out=codes[:].rearrange("p g n -> p (g n)").bitcast(FP8X4),
                scales=scales[:].rearrange("p g n -> p (g n)"),
                in_=u2_grp[i][:].rearrange("p g n t -> p (g n t)"),
            )
            u2_codes[i] = (codes, scales)

        w_codes = [keep.tile([P, 512], U32, name="w_codes%d" % c, align_bytes=64) for c in range(13)]
        w_scales = [keep.tile([P, 512], U8, name="w_scales%d" % c, align_bytes=64) for c in range(13)]
        w_grp = {}

        def copy_w(c):
            grp = pool.tile([P, 2048], BF16, name="w_grp", bufs=2, align_bytes=64)
            if c < 8:
                nc.vector.tensor_copy(
                    out=grp[:].rearrange("p (q t r j) -> p q t r j", q=4, t=8, j=4),
                    in_=w_raw[c][:].rearrange("p (t j r q) -> p q t r j", t=8, j=4, q=4),
                )
            else:
                nc.scalar.copy(
                    out=grp[:].rearrange("p (q m j) -> p q m j", q=4, j=4),
                    in_=w_raw[c][:].rearrange("p (j m q) -> p q m j", j=4, q=4),
                )
            w_grp[c] = grp

        def quant_w(c):
            nc.vector.quantize_mx(out=w_codes[c][:].bitcast(FP8X4), scales=w_scales[c][:], in_=w_grp[c][:])

        h_bank = {}
        h_grp = {}
        h_codes = [keep.tile([P, N], U32, name="h_codes%d" % g, align_bytes=64) for g in range(5)]
        h_scales = [keep.tile([P, N], U8, name="h_scales%d" % g, align_bytes=64) for g in range(5)]

        def multiply(group, t, lhs, passes=range(GD)):
            if (group, t // 2) not in h_bank:
                h_bank[group, t // 2] = psum.tile([P, 2, N], F32, name="hp", bufs=3)
            bank = h_bank[group, t // 2]
            for g in passes:
                codes, scales = lhs(g)
                nc.tensor.matmul_mx(
                    out=bank[:, t % 2, :],
                    lhsT=codes.bitcast(FP8X4),
                    lhsT_scale=scales,
                    rhs=x_codes[:, g, :].bitcast(FP8X4),
                    rhs_scale=x_scales[:, g, :],
                    start=(g == 0),
                    stop=(g == GD - 1),
                )

        def multiply_u2(i, passes=range(GD)):
            codes, scales = u2_codes[i]
            multiply(i // 4, i % 4, lambda g: (codes[:, g, :], scales[:, g, :]), passes)

        def multiply_s1(t):
            cols = slice(t * P, (t + 1) * P)
            multiply(4, t, lambda g: (w_codes[g][:, cols], w_scales[g][:, cols]))

        def empty_h(group, half):
            if half == 0:
                h_grp[group] = pool.tile([P, N, 4], BF16, name="h_grp", bufs=2, align_bytes=64)
            nc.scalar.copy(
                out=h_grp[group][:, :, 2 * half : 2 * half + 2],
                in_=h_bank[group, half][:].rearrange("p t n -> p n t"),
            )

        def quant_h(group):
            nc.vector.quantize_mx(
                out=h_codes[group][:].bitcast(FP8X4),
                scales=h_scales[group][:],
                in_=h_grp[group][:].rearrange("p n t -> p (n t)"),
            )

        a, b_, c_ = SEQ[:3]
        banks = [(SEQ[n // 4], n % 4) for n in range(4, 20)]
        for b in range(4):
            turn_u2(a, b)

        def head(g):
            turn_x(g)
            for i, b in banks[2 * g : 2 * g + 2]:
                turn_u2(i, b)

        head(0)
        head(1)
        head(2)
        quant_x(0)
        head(3)
        quant_u2(a)
        quant_x(1)
        multiply_u2(a, range(0, 2))
        head(4)
        multiply_u2(a, range(2, 4))
        head(5)
        quant_u2(b_)
        quant_x(2)
        load_u2(SEQ[5])
        head(6)
        multiply_u2(b_, range(0, 4))
        head(7)
        quant_u2(c_)
        quant_x(3)
        multiply_u2(a, range(4, 6))
        multiply_u2(b_, range(4, 6))
        multiply_u2(c_, range(0, 6))
        load_u2(SEQ[6])
        load_w(0)
        load_w(8)
        quant_u2(SEQ[3])
        for i in (a, b_, c_):
            multiply_u2(i, range(6, 8))
        copy_w(0)

        chunks = [0, 8, 1, 2, 9, 3, 4, 10, 5, 6, 11, 7, 12]
        at = 1
        copied = [0]
        group_done = []
        for s in range(3, TILES):
            load_w(chunks[at + 1]) if at + 1 < 13 else None
            if s + 4 < TILES:
                load_u2(SEQ[s + 4])
            if s + 2 < TILES:
                for b in range(4):
                    turn_u2(SEQ[s + 2], b)
            if s + 1 < TILES:
                quant_u2(SEQ[s + 1])
            if copied:
                quant_w(copied.pop())
            while group_done:
                quant_h(group_done.pop())
            if at < 13:
                copy_w(chunks[at])
                copied.append(chunks[at])
                at += 1
            if s == 15:
                for t in range(4):
                    multiply_s1(t)
                    if t % 2 == 1:
                        empty_h(4, t // 2)
            i = SEQ[s]
            multiply_u2(i)
            if i % 2 == 1:
                empty_h(i // 4, (i % 4) // 2)
                if i % 4 == 3:
                    group_done.append(i // 4)
        quant_h(4)
        quant_h(3)

        bias2 = const.tile([P, 4], F32, name="bias2", align_bytes=64)
        nc.vector.tensor_scalar(out=bias2[:], in0=bias_in[:], scalar1=2.0, scalar2=None, op0=MULT)
        order = [(4, 12), (0, 8), (1, 9), (2, 10), (3, 11)]
        acc = [psum.tile([P, 512], F32, name="tp", bufs=5) for m in range(4)]

        def second(m, n):
            group, w = order[n]
            nc.tensor.matmul_mx(
                out=acc[m][:, :N],
                lhsT=w_codes[w][:, m * P : (m + 1) * P].bitcast(FP8X4),
                lhsT_scale=w_scales[w][:, m * P : (m + 1) * P],
                rhs=h_codes[group][:].bitcast(FP8X4),
                rhs_scale=h_scales[group][:],
                start=(n == 0),
                stop=(n == 4),
            )

        for m in range(4):
            for n in range(4):
                second(m, n)
        result = keep.tile([P, 4, 4, 64], F32, name="result", align_bytes=64)
        out_view = out.rearrange("b (p m) i j -> p b m (i j)", m=4)
        for m in range(4):
            second(m, 4)
        for m in range(4):
            src = acc[m][:, :N].rearrange("p (b s) -> p b s", b=4)
            if m % 2 == 0:
                nc.scalar.activation(
                    out=result[:, :, m, :], in_=src, func=IDENTITY, bias=bias2[:, m : m + 1], scale=0.125
                )
            else:
                nc.vector.tensor_scalar(
                    out=result[:, :, m, :], in0=src, scalar1=0.125, scalar2=bias2[:, m : m + 1], op0=MULT, op1=ADD
                )
                nc.sync.dma_start(out=out_view[:, :, m - 1 : m + 1, :], in_=result[:, :, m - 1 : m + 1, :])
